import numpy as np
import ml_dtypes


def mxq(x, axis, fmt="e4m3"):
    dtype, down = {"e4m3": (ml_dtypes.float8_e4m3fn, 7), "e5m2": (ml_dtypes.float8_e5m2, 14)}[fmt]
    v = np.moveaxis(np.asarray(x, np.float32).astype(ml_dtypes.bfloat16).astype(np.float64), axis, -1)
    blocks = v.reshape(v.shape[:-1] + (-1, 32))
    amax = np.abs(blocks).max(-1, keepdims=True)
    byte = np.maximum(np.where(amax > 0, np.frexp(amax)[1] - 1 + 127, 0) - down, 1)
    scale = np.exp2(byte - 127.0)
    codes = (blocks / scale).astype(np.float32).astype(dtype).astype(np.float64)
    return np.moveaxis((codes * scale).reshape(v.shape), -1, axis)


WIDE = False


def mx_kscale(k):
    if not WIDE:
        return np.ones(k)
    levels = np.array([10, -10, 5, -5, 0])
    a = np.random.permutation(np.resize(levels, k // 512 * 4)).reshape(k // 512, 4)
    idx = np.arange(k)
    return np.exp2(a[idx // 512, idx % 128 // 32])


BF16 = ml_dtypes.bfloat16


def bf(x):
    return np.asarray(x, np.float32).astype(BF16)


def f64(x):
    return np.asarray(x).astype(np.float64)


E2M1 = np.array([0.0, 0.5, 1.0, 1.5, 2.0, 3.0, 4.0, 6.0, -0.0, -0.5, -1.0, -1.5, -2.0, -3.0, -4.0, -6.0])


def pack_weight(w, fmt):
    k, n = w.shape
    w = f64(bf(w)).reshape(k // 32, 32, n)
    amax = np.abs(w).max(1)
    if fmt == "e4m3":
        byte = np.frexp(amax)[1] - 1 + 127 - 7
    else:
        mant, ex = np.frexp(amax / 6.0)
        byte = np.where(mant > 0.5, ex, ex - 1) + 127
    byte = np.clip(np.where(amax > 0, byte, 1), 1, 254)
    scaled = (w * np.exp2(127.0 - byte)[:, None, :]).reshape(k, n).astype(np.float32)
    by_word = np.ascontiguousarray(scaled.reshape(k // 512, 128, 4, n).transpose(0, 1, 3, 2))
    if fmt == "e4m3":
        words = by_word.astype(ml_dtypes.float8_e4m3fn).view(np.uint8)
    else:
        c = by_word.astype(ml_dtypes.float4_e2m1fn).view(np.uint8) & 0xF
        words = c[..., 0::2] | (c[..., 1::2] << 4)
    return np.ascontiguousarray(words), np.ascontiguousarray(byte.astype(np.uint8).reshape(k // 512, 16, n))


def unpack_weight(words, scales, fmt):
    g, p, n, _ = words.shape
    if fmt == "e4m3":
        vals = np.ascontiguousarray(words).view(ml_dtypes.float8_e4m3fn).astype(np.float64)
    else:
        nib = np.empty((g, p, n, 4), np.uint8)
        nib[..., 0::2] = words & 0xF
        nib[..., 1::2] = words >> 4
        vals = E2M1[nib]
    vals = vals * np.repeat(np.exp2(scales.astype(np.float64) - 127.0), 8, axis=1)[..., None]
    return vals.transpose(0, 1, 3, 2).reshape(g * 512, n)

def pack4(w):
    words, scales = pack_weight(w, "e2m1")
    return words.reshape(words.shape[0], 128, -1), scales


def unpack4(words, scales):
    return unpack_weight(words.reshape(words.shape[0], 128, -1, 2), scales, "e2m1")


B, S, DIM, H, NOPE, ROPE_D, VD = 4, 1024, 1024, 2, 64, 64, 128
QKD = NOPE + ROPE_D
BASE = 10000.0


def rope_cos_sin(seq_len):
    theta = 1.0 / BASE ** (f64(np.arange(0, ROPE_D, 2)) / ROPE_D)
    pos = f64(np.arange(seq_len))
    ang = pos[:, None] * theta[None, :]
    return np.cos(ang), np.sin(ang)


def apply_rope(v, cos, sin):
    b, s, h, d = v.shape
    vs = v.reshape(b, s, h, d // 2, 2)
    c = cos[None, :, None, :]
    sn = sin[None, :, None, :]
    out = np.stack([vs[..., 0] * c - vs[..., 1] * sn, vs[..., 1] * c + vs[..., 0] * sn], axis=-1)
    return out.reshape(b, s, h, d)


def setup_inputs():
    s = mx_kscale(DIM)
    x = bf(np.random.standard_normal((B, S, DIM)) * s)
    Wq_words, Wq_scales = pack4(np.random.standard_normal((DIM, H * QKD)) / np.sqrt(DIM) / s[:, None])
    Wk_words, Wk_scales = pack4(np.random.standard_normal((DIM, H * QKD)) / np.sqrt(DIM) / s[:, None])
    return {'x': x,
            'Wq_words': Wq_words, 'Wq_scales': Wq_scales,
            'Wk_words': Wk_words, 'Wk_scales': Wk_scales}


def reference(x, Wq_words, Wq_scales, Wk_words, Wk_scales):
    xq = mxq(f64(x), 2, 'e4m3')
    q = (xq @ unpack4(Wq_words, Wq_scales)).reshape(B, S, H, QKD)
    k = (xq @ unpack4(Wk_words, Wk_scales)).reshape(B, S, H, QKD)
    cos, sin = rope_cos_sin(S)
    q = np.concatenate([q[..., :NOPE], apply_rope(q[..., NOPE:], cos, sin)], axis=-1)
    k = np.concatenate([k[..., :NOPE], apply_rope(k[..., NOPE:], cos, sin)], axis=-1)
    return q, k

@@ -1,0 +1,235 @@
+import math
+from contextlib import ExitStack
+
+import concourse.mybir as mybir
+from concourse.masks import make_identity
+
+F32 = mybir.dt.float32
+BF16 = mybir.dt.bfloat16
+I32 = mybir.dt.int32
+U32 = mybir.dt.uint32
+U8 = mybir.dt.uint8
+FP8X4 = mybir.dt.float8_e4m3fn_x4
+FP4X4 = mybir.dt.float4_e2m1fn_x4
+ALU = mybir.AluOpType
+ACT = mybir.ActivationFunctionType
+
+P = 128
+SEQS, SEQ_LEN, DIM = 4, 1024, 1024
+HEADS, NOPE, ROPE = 2, 64, 64
+COLS = HEADS * (NOPE + ROPE)
+FREQS = ROPE // 2
+BASE = 10000.0
+K_PASS = 4 * P
+PASSES = DIM // K_PASS
+WORDS = K_PASS // 2
+TILES_PER_SEQ = SEQ_LEN // P
+GROUP = 4
+GROUPS = SEQS * TILES_PER_SEQ // GROUP
+GROUPS_PER_SEQ = TILES_PER_SEQ // GROUP
+LOAD = 2
+QUANTISE = 2
+EARLY_LOADS = 4
+ROUND_MAGIC = 1.5 * 2.0**23
+
+FLOPS = 2 * SEQS * SEQ_LEN * DIM * 2 * COLS
+
+
+def rope_tables(nc, pool):
+    ratio = BASE ** (-2.0 / ROPE)
+    freq = pool.tile([P, FREQS], F32)
+    nc.vector.memset(freq[:, 0:1], 1.0)
+    for level in range(int(math.log2(FREQS))):
+        step = 2**level
+        nc.vector.tensor_scalar_mul(
+            out=freq[:, step : 2 * step], in0=freq[:, 0:step], scalar1=ratio**step
+        )
+
+    position_int = pool.tile([P, TILES_PER_SEQ], I32)
+    nc.gpsimd.iota(
+        position_int[:], pattern=[[1, TILES_PER_SEQ]], base=0, channel_multiplier=TILES_PER_SEQ
+    )
+    position = pool.tile([P, TILES_PER_SEQ], F32)
+    nc.vector.tensor_copy(out=position[:], in_=position_int[:])
+
+    shape = [P, TILES_PER_SEQ, FREQS]
+    turns = pool.tile(shape, F32)
+    nc.vector.scalar_tensor_tensor(
+        out=turns[:],
+        in0=position[:].unsqueeze(2).to_broadcast(shape),
+        scalar=1.0 / (2.0 * math.pi),
+        in1=freq[:].unsqueeze(1).to_broadcast(shape),
+        op0=ALU.mult,
+        op1=ALU.mult,
+    )
+    whole = pool.tile(shape, F32)
+    nc.vector.tensor_scalar(
+        out=whole[:],
+        in0=turns[:],
+        scalar1=ROUND_MAGIC,
+        scalar2=ROUND_MAGIC,
+        op0=ALU.add,
+        op1=ALU.subtract,
+    )
+    frac = pool.tile(shape, F32)
+    nc.vector.tensor_tensor(out=frac[:], in0=turns[:], in1=whole[:], op=ALU.subtract)
+    quarter = pool.tile(shape, F32)
+    nc.vector.scalar_tensor_tensor(
+        out=quarter[:], in0=frac[:], scalar=-1.0, in1=frac[:], op0=ALU.mult, op1=ALU.min
+    )
+    nc.vector.tensor_scalar_add(out=quarter[:], in0=quarter[:], scalar1=0.25)
+
+    sin = pool.tile(shape, F32)
+    nc.scalar.activation(out=sin[:], in_=frac[:], func=ACT.Sin, scale=2.0 * math.pi)
+    minus_sin = pool.tile(shape, F32)
+    nc.scalar.activation(out=minus_sin[:], in_=frac[:], func=ACT.Sin, scale=-2.0 * math.pi)
+    cos = pool.tile(shape + [2], F32)
+    nc.scalar.activation(
+        out=cos[:],
+        in_=quarter[:].unsqueeze(3).to_broadcast(shape + [2]),
+        func=ACT.Sin,
+        scale=2.0 * math.pi,
+    )
+    return cos, sin, minus_sin
+
+
+def tile_mla_pa_t_kernel(
+    tc, x, Wq_words, Wq_scales, Wk_words, Wk_scales, out_0, out_1
+):
+    nc = tc.nc
+    with ExitStack() as ctx:
+        consts = ctx.enter_context(tc.tile_pool(name="consts", bufs=1))
+        x_pool = ctx.enter_context(tc.tile_pool(name="x", bufs=GROUPS * GROUP // LOAD))
+        grouped_pool = ctx.enter_context(tc.tile_pool(name="grouped", bufs=2))
+        quantised_pool = ctx.enter_context(tc.tile_pool(name="quantised", bufs=2))
+        cross_pool = ctx.enter_context(tc.tile_pool(name="cross", bufs=GROUP))
+        out_pool = ctx.enter_context(tc.tile_pool(name="out", bufs=6))
+        transposed_psum = ctx.enter_context(tc.psum_pool(name="transposed", bufs=GROUP))
+        sums_psum = ctx.enter_context(tc.psum_pool(name="sums", bufs=GROUP))
+        ctx.enter_context(tc.manual_schedule())
+
+        def load_x(index):
+            seq, first = divmod(index * LOAD, TILES_PER_SEQ)
+            x_sb = x_pool.tile([P, LOAD, DIM], BF16, name="x_sb")
+            tiles = x[seq].rearrange("(p j) k -> p j k", j=TILES_PER_SEQ)
+            nc.sync.dma_start(out=x_sb[:], in_=tiles[:, first : first + LOAD, :])
+            return x_sb
+
+        x_loaded = [load_x(index) for index in range(EARLY_LOADS)]
+
+        w_words = consts.tile([P, PASSES, 2 * 2 * COLS], U8, align_bytes=64)
+        w_scales = consts.tile([P, PASSES, 2 * COLS], U8, align_bytes=64)
+        nc.vector.memset(w_scales[:].bitcast(I32), 0)
+        for side, words in enumerate((Wq_words, Wk_words)):
+            nc.sync.dma_start(
+                out=w_words[:, :, side * 2 * COLS : (side + 1) * 2 * COLS].bitcast(I32),
+                in_=words.rearrange("g p n -> p g n").bitcast(I32),
+            )
+        for side, scales in enumerate((Wq_scales, Wk_scales)):
+            for quadrant in range(4):
+                nc.sync.dma_start(
+                    out=w_scales[
+                        32 * quadrant : 32 * quadrant + 4, :, side * COLS : (side + 1) * COLS
+                    ].bitcast(I32),
+                    in_=scales[:, 4 * quadrant : 4 * quadrant + 4, :]
+                    .rearrange("g r n -> r g n")
+                    .bitcast(I32),
+                )
+
+        x_loaded.extend(load_x(index) for index in range(EARLY_LOADS, GROUPS * GROUP // LOAD))
+
+        cos, sin, minus_sin = rope_tables(nc, consts)
+        identity = consts.tile([P, P], F32)
+        make_identity(nc, identity[:])
+
+        def transpose_and_quantise(group):
+            grouped = grouped_pool.tile([P, GROUP, DIM], BF16, align_bytes=64, name="grouped")
+            for t in range(GROUP):
+                index, part = divmod(group * GROUP + t, LOAD)
+                x_words = x_loaded[index][:, part, :].bitcast(F32)
+                transposed = transposed_psum.tile([P, PASSES, 2, P], F32, name="transposed")
+                for g in range(PASSES):
+                    for u in range(2):
+                        nc.tensor.transpose(
+                            transposed[:, g, u, :],
+                            x_words[:, g * WORDS + u : (g + 1) * WORDS : 2],
+                            identity[:],
+                        )
+                nc.scalar.copy(
+                    out=grouped[:, t, :]
+                    .bitcast(F32)
+                    .rearrange("p (g r u) -> p g r u", g=PASSES, u=2),
+                    in_=transposed[:].rearrange("p g u r -> p g r u"),
+                )
+            codes = quantised_pool.tile([P, GROUP * PASSES * P], U32, align_bytes=64, name="codes")
+            scales = quantised_pool.tile([P, GROUP * PASSES * P], U8, align_bytes=64, name="scales")
+            for first in range(0, GROUP, QUANTISE):
+                cols = slice(first * PASSES * P, (first + QUANTISE) * PASSES * P)
+                nc.vector.quantize_mx(
+                    out=codes[:, cols].bitcast(FP8X4),
+                    scales=scales[:, cols],
+                    in_=grouped[:, first : first + QUANTISE, :].rearrange("p t k -> p (t k)"),
+                )
+            return codes, scales
+
+        def multiply_and_rotate(group, codes, scales):
+            seq, part = divmod(group, GROUPS_PER_SEQ)
+            out_sb = out_pool.tile([P, 2, GROUP, COLS], F32, name="out_sb")
+            for t in range(GROUP):
+                sums = sums_psum.tile([P, 2 * COLS], F32, name="sums")
+                for g in range(PASSES):
+                    cols = slice((t * PASSES + g) * P, (t * PASSES + g + 1) * P)
+                    nc.tensor.matmul_mx(
+                        out=sums[:],
+                        lhsT=codes[:, cols].bitcast(FP8X4),
+                        lhsT_scale=scales[:, cols],
+                        rhs=w_words[:, g, :].bitcast(FP4X4),
+                        rhs_scale=w_scales[:, g, :],
+                        start=(g == 0),
+                        stop=(g == PASSES - 1),
+                    )
+                src = sums[:].rearrange("p (q h s c) -> p q h s c", q=2, h=HEADS, s=2)
+                dst = out_sb[:, :, t, :].rearrange("p q (h s c) -> p q h s c", h=HEADS, s=2)
+                nc.scalar.copy(out=dst[:, :, :, 0, :], in_=src[:, :, :, 0, :])
+
+                j = part * GROUP + t
+                heads = [P, 2, HEADS]
+                nc.vector.tensor_tensor(
+                    out=dst[:, :, :, 1, :],
+                    in0=src[:, :, :, 1, :],
+                    in1=cos[:, j, :, :]
+                    .rearrange("p i e -> p (i e)")
+                    .unsqueeze(1)
+                    .unsqueeze(1)
+                    .to_broadcast(heads + [ROPE]),
+                    op=ALU.mult,
+                )
+                src_pairs = src[:, :, :, 1, :].rearrange("p q h (i e) -> p q h i e", e=2)
+                dst_pairs = dst[:, :, :, 1, :].rearrange("p q h (i e) -> p q h i e", e=2)
+                cross = cross_pool.tile([P, 2, 2, HEADS, FREQS], F32, name="cross")
+                for e, table in enumerate((minus_sin, sin)):
+                    nc.vector.tensor_tensor(
+                        out=cross[:, e, :, :, :],
+                        in0=src_pairs[:, :, :, :, 1 - e],
+                        in1=table[:, j, :].unsqueeze(1).unsqueeze(1).to_broadcast(heads + [FREQS]),
+                        op=ALU.mult,
+                    )
+                nc.gpsimd.tensor_tensor(
+                    out=dst_pairs,
+                    in0=dst_pairs,
+                    in1=cross[:].rearrange("p e q h i -> p q h i e"),
+                    op=ALU.add,
+                )
+            rows = slice(part * GROUP, (part + 1) * GROUP)
+            for side, out in enumerate((out_0, out_1)):
+                nc.sync.dma_start(
+                    out=out[seq].rearrange("(p j) h d -> p j (h d)", j=TILES_PER_SEQ)[:, rows, :],
+                    in_=out_sb[:, side, :, :],
+                )
+
+        quantised = transpose_and_quantise(0)
+        for group in range(1, GROUPS):
+            following = transpose_and_quantise(group)
+            multiply_and_rotate(group - 1, quantised[0], quantised[1])
+            quantised = following
+        multiply_and_rotate(GROUPS - 1, quantised[0], quantised[1])

@@ -35,7 +35,7 @@ ROUND_MAGIC = 1.5 * 2.0**23
 FLOPS = 2 * SEQS * SEQ_LEN * DIM * 2 * COLS
 
 
-def rope_tables(nc, pool):
+def rope_angles(nc, pool):
     ratio = BASE ** (-2.0 / ROPE)
     freq = pool.tile([P, FREQS], F32)
     nc.vector.memset(freq[:, 0:1], 1.0)
@@ -71,26 +71,26 @@ def rope_tables(nc, pool):
         op0=ALU.add,
         op1=ALU.subtract,
     )
-    frac = pool.tile(shape, F32)
-    nc.vector.tensor_tensor(out=frac[:], in0=turns[:], in1=whole[:], op=ALU.subtract)
-    quarter = pool.tile(shape, F32)
-    nc.vector.scalar_tensor_tensor(
-        out=quarter[:], in0=frac[:], scalar=-1.0, in1=frac[:], op0=ALU.mult, op1=ALU.min
+    turns_of = pool.tile([P, 2] + shape[1:] + [2], F32)
+    frac = turns_of[:, 1, :, :, 1]
+    nc.vector.tensor_tensor(out=frac, in0=turns[:], in1=whole[:], op=ALU.subtract)
+    nc.vector.tensor_tensor(out=turns_of[:, 1, :, :, 0], in0=whole[:], in1=turns[:], op=ALU.subtract)
+    minus_abs = pool.tile(shape, F32)
+    nc.vector.tensor_tensor(
+        out=minus_abs[:], in0=frac, in1=turns_of[:, 1, :, :, 0], op=ALU.min
     )
-    nc.vector.tensor_scalar_add(out=quarter[:], in0=quarter[:], scalar1=0.25)
+    nc.vector.tensor_scalar_add(
+        out=turns_of[:, 0, :, :, :],
+        in0=minus_abs[:].unsqueeze(3).to_broadcast(shape + [2]),
+        scalar1=0.25,
+    )
+    return turns_of
 
-    sin = pool.tile(shape, F32)
-    nc.scalar.activation(out=sin[:], in_=frac[:], func=ACT.Sin, scale=2.0 * math.pi)
-    minus_sin = pool.tile(shape, F32)
-    nc.scalar.activation(out=minus_sin[:], in_=frac[:], func=ACT.Sin, scale=-2.0 * math.pi)
-    cos = pool.tile(shape + [2], F32)
-    nc.scalar.activation(
-        out=cos[:],
-        in_=quarter[:].unsqueeze(3).to_broadcast(shape + [2]),
-        func=ACT.Sin,
-        scale=2.0 * math.pi,
-    )
-    return cos, sin, minus_sin
+
+def rope_tables(nc, pool, turns_of):
+    tables = pool.tile([P, 2, TILES_PER_SEQ, FREQS, 2], F32)
+    nc.scalar.activation(out=tables[:], in_=turns_of[:], func=ACT.Sin, scale=2.0 * math.pi)
+    return tables[:, 0, :, :, :], tables[:, 1, :, :, :]
 
 
 def tile_mla_pa_t_kernel(
@@ -138,7 +138,10 @@ def tile_mla_pa_t_kernel(
 
         x_loaded.extend(load_x(index) for index in range(EARLY_LOADS, GROUPS * GROUP // LOAD))
 
-        cos, sin, minus_sin = rope_tables(nc, consts)
+        warm = consts.tile([P, 2], F32)
+        nc.vector.memset(warm[:, 0:1], 0.0)
+        nc.scalar.activation(out=warm[:, 1:2], in_=warm[:, 0:1], func=ACT.Sin)
+        turns_of = rope_angles(nc, consts)
         identity = consts.tile([P, P], F32)
         make_identity(nc, identity[:])
 
@@ -174,7 +177,17 @@ def tile_mla_pa_t_kernel(
 
         def multiply_and_rotate(group, codes, scales):
             seq, part = divmod(group, GROUPS_PER_SEQ)
+            last_group = group == GROUPS - 1
             out_sb = out_pool.tile([P, 2, GROUP, COLS], F32, name="out_sb")
+
+            def store(first, count):
+                rows = slice(part * GROUP + first, part * GROUP + first + count)
+                for side, out in enumerate((out_0, out_1)):
+                    nc.sync.dma_start(
+                        out=out[seq].rearrange("(p j) h d -> p j (h d)", j=TILES_PER_SEQ)[:, rows, :],
+                        in_=out_sb[:, side, first : first + count, :],
+                    )
+
             for t in range(GROUP):
                 sums = sums_psum.tile([P, 2 * COLS], F32, name="sums")
                 for g in range(PASSES):
@@ -205,29 +218,30 @@ def tile_mla_pa_t_kernel(
                     op=ALU.mult,
                 )
                 src_pairs = src[:, :, :, 1, :].rearrange("p q h (i e) -> p q h i e", e=2)
-                dst_pairs = dst[:, :, :, 1, :].rearrange("p q h (i e) -> p q h i e", e=2)
-                cross = cross_pool.tile([P, 2, 2, HEADS, FREQS], F32, name="cross")
-                for e, table in enumerate((minus_sin, sin)):
-                    nc.vector.tensor_tensor(
-                        out=cross[:, e, :, :, :],
-                        in0=src_pairs[:, :, :, :, 1 - e],
-                        in1=table[:, j, :].unsqueeze(1).unsqueeze(1).to_broadcast(heads + [FREQS]),
-                        op=ALU.mult,
-                    )
-                nc.gpsimd.tensor_tensor(
-                    out=dst_pairs,
-                    in0=dst_pairs,
-                    in1=cross[:].rearrange("p e q h i -> p q h i e"),
+                cross = cross_pool.tile([P, 2, HEADS, FREQS, 2], F32, name="cross")
+                nc.vector.tensor_tensor(
+                    out=cross[:],
+                    in0=src_pairs[:, :, :, :, ::-1],
+                    in1=signed_sin[:, j, :, :]
+                    .unsqueeze(1)
+                    .unsqueeze(1)
+                    .to_broadcast(heads + [FREQS, 2]),
+                    op=ALU.mult,
+                )
+                adder = nc.vector if last_group and t == GROUP - 1 else nc.gpsimd
+                adder.tensor_tensor(
+                    out=dst[:, :, :, 1, :],
+                    in0=dst[:, :, :, 1, :],
+                    in1=cross[:].rearrange("p q h i e -> p q h (i e)"),
                     op=ALU.add,
                 )
-            rows = slice(part * GROUP, (part + 1) * GROUP)
-            for side, out in enumerate((out_0, out_1)):
-                nc.sync.dma_start(
-                    out=out[seq].rearrange("(p j) h d -> p j (h d)", j=TILES_PER_SEQ)[:, rows, :],
-                    in_=out_sb[:, side, :, :],
-                )
+                if last_group:
+                    store(t, 1)
+            if not last_group:
+                store(0, GROUP)
 
         quantised = transpose_and_quantise(0)
+        cos, signed_sin = rope_tables(nc, consts, turns_of)
         for group in range(1, GROUPS):
             following = transpose_and_quantise(group)
             multiply_and_rotate(group - 1, quantised[0], quantised[1])

@@ -30,6 +30,7 @@ GROUPS_PER_SEQ = TILES_PER_SEQ // GROUP
 LOAD = 2
 QUANTISE = 2
 EARLY_LOADS = 4
+GPSIMD_ADDS = 2
 ROUND_MAGIC = 1.5 * 2.0**23
 
 FLOPS = 2 * SEQS * SEQ_LEN * DIM * 2 * COLS
@@ -188,6 +189,8 @@ def tile_mla_pa_t_kernel(
                         in_=out_sb[:, side, first : first + count, :],
                     )
 
+            gpsimd_adds = GROUP - 1 if last_group else GPSIMD_ADDS
+            left_to_add = []
             for t in range(GROUP):
                 sums = sums_psum.tile([P, 2 * COLS], F32, name="sums")
                 for g in range(PASSES):
@@ -228,10 +231,21 @@ def tile_mla_pa_t_kernel(
                     .to_broadcast(heads + [FREQS, 2]),
                     op=ALU.mult,
                 )
-                adder = nc.vector if last_group and t == GROUP - 1 else nc.gpsimd
-                adder.tensor_tensor(
-                    out=dst[:, :, :, 1, :],
-                    in0=dst[:, :, :, 1, :],
+                if t < gpsimd_adds:
+                    nc.gpsimd.tensor_tensor(
+                        out=dst[:, :, :, 1, :],
+                        in0=dst[:, :, :, 1, :],
+                        in1=cross[:].rearrange("p q h i e -> p q h (i e)"),
+                        op=ALU.add,
+                    )
+                    if last_group:
+                        store(t, 1)
+                else:
+                    left_to_add.append((t, dst[:, :, :, 1, :], cross))
+            for t, rotated, cross in left_to_add:
+                nc.vector.tensor_tensor(
+                    out=rotated,
+                    in0=rotated,
                     in1=cross[:].rearrange("p q h i e -> p q h (i e)"),
                     op=ALU.add,
                 )

@@ -31,6 +31,8 @@ LOAD = 2
 QUANTISE = 2
 EARLY_LOADS = 4
 GPSIMD_ADDS = 2
+FIRST_SORTED = 3
+SORTED_TILE = 3
 ROUND_MAGIC = 1.5 * 2.0**23
 
 FLOPS = 2 * SEQS * SEQ_LEN * DIM * 2 * COLS
@@ -103,6 +105,7 @@ def tile_mla_pa_t_kernel(
         x_pool = ctx.enter_context(tc.tile_pool(name="x", bufs=GROUPS * GROUP // LOAD))
         grouped_pool = ctx.enter_context(tc.tile_pool(name="grouped", bufs=2))
         quantised_pool = ctx.enter_context(tc.tile_pool(name="quantised", bufs=2))
+        sorted_pool = ctx.enter_context(tc.tile_pool(name="sorted", bufs=2))
         cross_pool = ctx.enter_context(tc.tile_pool(name="cross", bufs=GROUP))
         out_pool = ctx.enter_context(tc.tile_pool(name="out", bufs=6))
         transposed_psum = ctx.enter_context(tc.psum_pool(name="transposed", bufs=GROUP))
@@ -146,17 +149,33 @@ def tile_mla_pa_t_kernel(
         identity = consts.tile([P, P], F32)
         make_identity(nc, identity[:])
 
+        def words_of(group, t):
+            index, part = divmod(group * GROUP + t, LOAD)
+            return x_loaded[index][:, part, :].bitcast(F32)
+
+        sorted_words = {}
+
+        def sort_words(group, t):
+            if FIRST_SORTED <= group < GROUPS:
+                in_order = sorted_pool.tile([P, PASSES, 2, P], F32, name="in_order")
+                nc.scalar.copy(
+                    out=in_order[:],
+                    in_=words_of(group, t).rearrange("p (g m u) -> p g u m", g=PASSES, u=2),
+                )
+                sorted_words[(group, t)] = in_order
+
         def transpose_and_quantise(group):
             grouped = grouped_pool.tile([P, GROUP, DIM], BF16, align_bytes=64, name="grouped")
             for t in range(GROUP):
-                index, part = divmod(group * GROUP + t, LOAD)
-                x_words = x_loaded[index][:, part, :].bitcast(F32)
+                x_words = words_of(group, t)
                 transposed = transposed_psum.tile([P, PASSES, 2, P], F32, name="transposed")
                 for g in range(PASSES):
                     for u in range(2):
                         nc.tensor.transpose(
                             transposed[:, g, u, :],
-                            x_words[:, g * WORDS + u : (g + 1) * WORDS : 2],
+                            sorted_words[(group, t)][:, g, u, :]
+                            if (group, t) in sorted_words
+                            else x_words[:, g * WORDS + u : (g + 1) * WORDS : 2],
                             identity[:],
                         )
                 nc.scalar.copy(
@@ -165,6 +184,7 @@ def tile_mla_pa_t_kernel(
                     .rearrange("p (g r u) -> p g r u", g=PASSES, u=2),
                     in_=transposed[:].rearrange("p g u r -> p g r u"),
                 )
+            sort_words(group + 1, SORTED_TILE)
             codes = quantised_pool.tile([P, GROUP * PASSES * P], U32, align_bytes=64, name="codes")
             scales = quantised_pool.tile([P, GROUP * PASSES * P], U8, align_bytes=64, name="scales")
             for first in range(0, GROUP, QUANTISE):

@@ -28,10 +28,10 @@ GROUP = 4
 GROUPS = SEQS * TILES_PER_SEQ // GROUP
 GROUPS_PER_SEQ = TILES_PER_SEQ // GROUP
 LOAD = 2
-QUANTISE = 2
+QUANTISE = 1
 EARLY_LOADS = 4
 GPSIMD_ADDS = 2
-FIRST_SORTED = 3
+FIRST_SORTED = 2
 SORTED_TILE = 3
 ROUND_MAGIC = 1.5 * 2.0**23
 
@@ -155,14 +155,17 @@ def tile_mla_pa_t_kernel(
 
         sorted_words = {}
 
-        def sort_words(group, t):
+        def sort_words(group, t, g):
             if FIRST_SORTED <= group < GROUPS:
-                in_order = sorted_pool.tile([P, PASSES, 2, P], F32, name="in_order")
+                if g == 0:
+                    in_order = sorted_pool.tile([P, PASSES, 2, P], F32, name="in_order")
+                    sorted_words[(group, t)] = in_order
                 nc.scalar.copy(
-                    out=in_order[:],
-                    in_=words_of(group, t).rearrange("p (g m u) -> p g u m", g=PASSES, u=2),
+                    out=sorted_words[(group, t)][:, g, :, :],
+                    in_=words_of(group, t)[:, g * WORDS : (g + 1) * WORDS].rearrange(
+                        "p (m u) -> p u m", u=2
+                    ),
                 )
-                sorted_words[(group, t)] = in_order
 
         def transpose_and_quantise(group):
             grouped = grouped_pool.tile([P, GROUP, DIM], BF16, align_bytes=64, name="grouped")
@@ -184,7 +187,6 @@ def tile_mla_pa_t_kernel(
                     .rearrange("p (g r u) -> p g r u", g=PASSES, u=2),
                     in_=transposed[:].rearrange("p g u r -> p g r u"),
                 )
-            sort_words(group + 1, SORTED_TILE)
             codes = quantised_pool.tile([P, GROUP * PASSES * P], U32, align_bytes=64, name="codes")
             scales = quantised_pool.tile([P, GROUP * PASSES * P], U8, align_bytes=64, name="scales")
             for first in range(0, GROUP, QUANTISE):
@@ -227,6 +229,8 @@ def tile_mla_pa_t_kernel(
                 src = sums[:].rearrange("p (q h s c) -> p q h s c", q=2, h=HEADS, s=2)
                 dst = out_sb[:, :, t, :].rearrange("p q (h s c) -> p q h s c", h=HEADS, s=2)
                 nc.scalar.copy(out=dst[:, :, :, 0, :], in_=src[:, :, :, 0, :])
+                if t >= GROUP - PASSES:
+                    sort_words(group + 2, SORTED_TILE, t - (GROUP - PASSES))
 
                 j = part * GROUP + t
                 heads = [P, 2, HEADS]

@@ -33,6 +33,7 @@ EARLY_LOADS = 4
 GPSIMD_ADDS = 2
 FIRST_SORTED = 2
 SORTED_TILE = 3
+WARMING_MATMULS = 3
 ROUND_MAGIC = 1.5 * 2.0**23
 
 FLOPS = 2 * SEQS * SEQ_LEN * DIM * 2 * COLS
@@ -282,6 +283,16 @@ def tile_mla_pa_t_kernel(
         cos, signed_sin = rope_tables(nc, consts, turns_of)
         for group in range(1, GROUPS):
             following = transpose_and_quantise(group)
+            if group == 1:
+                unread = sums_psum.tile([P, 2 * COLS], F32, name="sums")
+                for repeat in range(WARMING_MATMULS):
+                    nc.tensor.matmul(
+                        out=unread[:],
+                        lhsT=x_loaded[0][:, 0, 0:P],
+                        rhs=x_loaded[0][:, 0, 0 : 2 * COLS],
+                        start=True,
+                        stop=True,
+                    )
             multiply_and_rotate(group - 1, quantised[0], quantised[1])
             quantised = following
         multiply_and_rotate(GROUPS - 1, quantised[0], quantised[1])

@@ -120,17 +120,11 @@ def tile_mla_pa_t_kernel(
             nc.sync.dma_start(out=x_sb[:], in_=tiles[:, first : first + LOAD, :])
             return x_sb
 
-        x_loaded = [load_x(index) for index in range(EARLY_LOADS)]
-
         w_words = consts.tile([P, PASSES, 2 * 2 * COLS], U8, align_bytes=64)
         w_scales = consts.tile([P, PASSES, 2 * COLS], U8, align_bytes=64)
         nc.vector.memset(w_scales[:].bitcast(I32), 0)
-        for side, words in enumerate((Wq_words, Wk_words)):
-            nc.sync.dma_start(
-                out=w_words[:, :, side * 2 * COLS : (side + 1) * 2 * COLS].bitcast(I32),
-                in_=words.rearrange("g p n -> p g n").bitcast(I32),
-            )
-        for side, scales in enumerate((Wq_scales, Wk_scales)):
+
+        def load_scales(side, scales):
             for quadrant in range(4):
                 nc.sync.dma_start(
                     out=w_scales[
@@ -140,6 +134,16 @@ def tile_mla_pa_t_kernel(
                     .rearrange("g r n -> r g n")
                     .bitcast(I32),
                 )
+
+        x_loaded = [load_x(0)]
+        load_scales(0, Wq_scales)
+        x_loaded.extend(load_x(index) for index in range(1, EARLY_LOADS))
+        load_scales(1, Wk_scales)
+        for side, words in enumerate((Wq_words, Wk_words)):
+            nc.sync.dma_start(
+                out=w_words[:, :, side * 2 * COLS : (side + 1) * 2 * COLS].bitcast(I32),
+                in_=words.rearrange("g p n -> p g n").bitcast(I32),
+            )
 
         x_loaded.extend(load_x(index) for index in range(EARLY_LOADS, GROUPS * GROUP // LOAD))
 

import math
from contextlib import ExitStack

import concourse.mybir as mybir
from concourse.masks import make_identity

F32 = mybir.dt.float32
BF16 = mybir.dt.bfloat16
I32 = mybir.dt.int32
U32 = mybir.dt.uint32
U8 = mybir.dt.uint8
FP8X4 = mybir.dt.float8_e4m3fn_x4
FP4X4 = mybir.dt.float4_e2m1fn_x4
ALU = mybir.AluOpType
ACT = mybir.ActivationFunctionType

P = 128
SEQS, SEQ_LEN, DIM = 4, 1024, 1024
HEADS, NOPE, ROPE = 2, 64, 64
COLS = HEADS * (NOPE + ROPE)
FREQS = ROPE // 2
BASE = 10000.0
K_PASS = 4 * P
PASSES = DIM // K_PASS
WORDS = K_PASS // 2
TILES_PER_SEQ = SEQ_LEN // P
GROUP = 4
GROUPS = SEQS * TILES_PER_SEQ // GROUP
GROUPS_PER_SEQ = TILES_PER_SEQ // GROUP
LOAD = 2
QUANTISE = 1
EARLY_LOADS = 4
GPSIMD_ADDS = 2
FIRST_SORTED = 2
SORTED_TILE = 3
WARMING_MATMULS = 3
ROUND_MAGIC = 1.5 * 2.0**23

FLOPS = 2 * SEQS * SEQ_LEN * DIM * 2 * COLS


def rope_angles(nc, pool):
    ratio = BASE ** (-2.0 / ROPE)
    freq = pool.tile([P, FREQS], F32)
    nc.vector.memset(freq[:, 0:1], 1.0)
    for level in range(int(math.log2(FREQS))):
        step = 2**level
        nc.vector.tensor_scalar_mul(
            out=freq[:, step : 2 * step], in0=freq[:, 0:step], scalar1=ratio**step
        )

    position_int = pool.tile([P, TILES_PER_SEQ], I32)
    nc.gpsimd.iota(
        position_int[:], pattern=[[1, TILES_PER_SEQ]], base=0, channel_multiplier=TILES_PER_SEQ
    )
    position = pool.tile([P, TILES_PER_SEQ], F32)
    nc.vector.tensor_copy(out=position[:], in_=position_int[:])

    shape = [P, TILES_PER_SEQ, FREQS]
    turns = pool.tile(shape, F32)
    nc.vector.scalar_tensor_tensor(
        out=turns[:],
        in0=position[:].unsqueeze(2).to_broadcast(shape),
        scalar=1.0 / (2.0 * math.pi),
        in1=freq[:].unsqueeze(1).to_broadcast(shape),
        op0=ALU.mult,
        op1=ALU.mult,
    )
    whole = pool.tile(shape, F32)
    nc.vector.tensor_scalar(
        out=whole[:],
        in0=turns[:],
        scalar1=ROUND_MAGIC,
        scalar2=ROUND_MAGIC,
        op0=ALU.add,
        op1=ALU.subtract,
    )
    turns_of = pool.tile([P, 2] + shape[1:] + [2], F32)
    frac = turns_of[:, 1, :, :, 1]
    nc.vector.tensor_tensor(out=frac, in0=turns[:], in1=whole[:], op=ALU.subtract)
    nc.vector.tensor_tensor(out=turns_of[:, 1, :, :, 0], in0=whole[:], in1=turns[:], op=ALU.subtract)
    minus_abs = pool.tile(shape, F32)
    nc.vector.tensor_tensor(
        out=minus_abs[:], in0=frac, in1=turns_of[:, 1, :, :, 0], op=ALU.min
    )
    nc.vector.tensor_scalar_add(
        out=turns_of[:, 0, :, :, :],
        in0=minus_abs[:].unsqueeze(3).to_broadcast(shape + [2]),
        scalar1=0.25,
    )
    return turns_of


def rope_tables(nc, pool, turns_of):
    tables = pool.tile([P, 2, TILES_PER_SEQ, FREQS, 2], F32)
    nc.scalar.activation(out=tables[:], in_=turns_of[:], func=ACT.Sin, scale=2.0 * math.pi)
    return tables[:, 0, :, :, :], tables[:, 1, :, :, :]


def tile_mla_pa_t_kernel(
    tc, x, Wq_words, Wq_scales, Wk_words, Wk_scales, out_0, out_1
):
    nc = tc.nc
    with ExitStack() as ctx:
        consts = ctx.enter_context(tc.tile_pool(name="consts", bufs=1))
        x_pool = ctx.enter_context(tc.tile_pool(name="x", bufs=GROUPS * GROUP // LOAD))
        grouped_pool = ctx.enter_context(tc.tile_pool(name="grouped", bufs=2))
        quantised_pool = ctx.enter_context(tc.tile_pool(name="quantised", bufs=2))
        sorted_pool = ctx.enter_context(tc.tile_pool(name="sorted", bufs=2))
        cross_pool = ctx.enter_context(tc.tile_pool(name="cross", bufs=GROUP))
        out_pool = ctx.enter_context(tc.tile_pool(name="out", bufs=6))
        transposed_psum = ctx.enter_context(tc.psum_pool(name="transposed", bufs=GROUP))
        sums_psum = ctx.enter_context(tc.psum_pool(name="sums", bufs=GROUP))
        ctx.enter_context(tc.manual_schedule())

        def load_x(index):
            seq, first = divmod(index * LOAD, TILES_PER_SEQ)
            x_sb = x_pool.tile([P, LOAD, DIM], BF16, name="x_sb")
            tiles = x[seq].rearrange("(p j) k -> p j k", j=TILES_PER_SEQ)
            nc.sync.dma_start(out=x_sb[:], in_=tiles[:, first : first + LOAD, :])
            return x_sb

        w_words = consts.tile([P, PASSES, 2 * 2 * COLS], U8, align_bytes=64)
        w_scales = consts.tile([P, PASSES, 2 * COLS], U8, align_bytes=64)
        nc.vector.memset(w_scales[:].bitcast(I32), 0)

        def load_scales(side, scales):
            for quadrant in range(4):
                nc.sync.dma_start(
                    out=w_scales[
                        32 * quadrant : 32 * quadrant + 4, :, side * COLS : (side + 1) * COLS
                    ].bitcast(I32),
                    in_=scales[:, 4 * quadrant : 4 * quadrant + 4, :]
                    .rearrange("g r n -> r g n")
                    .bitcast(I32),
                )

        x_loaded = [load_x(0)]
        load_scales(0, Wq_scales)
        x_loaded.extend(load_x(index) for index in range(1, EARLY_LOADS))
        load_scales(1, Wk_scales)
        for side, words in enumerate((Wq_words, Wk_words)):
            nc.sync.dma_start(
                out=w_words[:, :, side * 2 * COLS : (side + 1) * 2 * COLS].bitcast(I32),
                in_=words.rearrange("g p n -> p g n").bitcast(I32),
            )

        x_loaded.extend(load_x(index) for index in range(EARLY_LOADS, GROUPS * GROUP // LOAD))

        warm = consts.tile([P, 2], F32)
        nc.vector.memset(warm[:, 0:1], 0.0)
        nc.scalar.activation(out=warm[:, 1:2], in_=warm[:, 0:1], func=ACT.Sin)
        turns_of = rope_angles(nc, consts)
        identity = consts.tile([P, P], F32)
        make_identity(nc, identity[:])

        def words_of(group, t):
            index, part = divmod(group * GROUP + t, LOAD)
            return x_loaded[index][:, part, :].bitcast(F32)

        sorted_words = {}

        def sort_words(group, t, g):
            if FIRST_SORTED <= group < GROUPS:
                if g == 0:
                    in_order = sorted_pool.tile([P, PASSES, 2, P], F32, name="in_order")
                    sorted_words[(group, t)] = in_order
                nc.scalar.copy(
                    out=sorted_words[(group, t)][:, g, :, :],
                    in_=words_of(group, t)[:, g * WORDS : (g + 1) * WORDS].rearrange(
                        "p (m u) -> p u m", u=2
                    ),
                )

        def transpose_and_quantise(group):
            grouped = grouped_pool.tile([P, GROUP, DIM], BF16, align_bytes=64, name="grouped")
            for t in range(GROUP):
                x_words = words_of(group, t)
                transposed = transposed_psum.tile([P, PASSES, 2, P], F32, name="transposed")
                for g in range(PASSES):
                    for u in range(2):
                        nc.tensor.transpose(
                            transposed[:, g, u, :],
                            sorted_words[(group, t)][:, g, u, :]
                            if (group, t) in sorted_words
                            else x_words[:, g * WORDS + u : (g + 1) * WORDS : 2],
                            identity[:],
                        )
                nc.scalar.copy(
                    out=grouped[:, t, :]
                    .bitcast(F32)
                    .rearrange("p (g r u) -> p g r u", g=PASSES, u=2),
                    in_=transposed[:].rearrange("p g u r -> p g r u"),
                )
            codes = quantised_pool.tile([P, GROUP * PASSES * P], U32, align_bytes=64, name="codes")
            scales = quantised_pool.tile([P, GROUP * PASSES * P], U8, align_bytes=64, name="scales")
            for first in range(0, GROUP, QUANTISE):
                cols = slice(first * PASSES * P, (first + QUANTISE) * PASSES * P)
                nc.vector.quantize_mx(
                    out=codes[:, cols].bitcast(FP8X4),
                    scales=scales[:, cols],
                    in_=grouped[:, first : first + QUANTISE, :].rearrange("p t k -> p (t k)"),
                )
            return codes, scales

        def multiply_and_rotate(group, codes, scales):
            seq, part = divmod(group, GROUPS_PER_SEQ)
            last_group = group == GROUPS - 1
            out_sb = out_pool.tile([P, 2, GROUP, COLS], F32, name="out_sb")

            def store(first, count):
                rows = slice(part * GROUP + first, part * GROUP + first + count)
                for side, out in enumerate((out_0, out_1)):
                    nc.sync.dma_start(
                        out=out[seq].rearrange("(p j) h d -> p j (h d)", j=TILES_PER_SEQ)[:, rows, :],
                        in_=out_sb[:, side, first : first + count, :],
                    )

            gpsimd_adds = GROUP - 1 if last_group else GPSIMD_ADDS
            left_to_add = []
            for t in range(GROUP):
                sums = sums_psum.tile([P, 2 * COLS], F32, name="sums")
                for g in range(PASSES):
                    cols = slice((t * PASSES + g) * P, (t * PASSES + g + 1) * P)
                    nc.tensor.matmul_mx(
                        out=sums[:],
                        lhsT=codes[:, cols].bitcast(FP8X4),
                        lhsT_scale=scales[:, cols],
                        rhs=w_words[:, g, :].bitcast(FP4X4),
                        rhs_scale=w_scales[:, g, :],
                        start=(g == 0),
                        stop=(g == PASSES - 1),
                    )
                src = sums[:].rearrange("p (q h s c) -> p q h s c", q=2, h=HEADS, s=2)
                dst = out_sb[:, :, t, :].rearrange("p q (h s c) -> p q h s c", h=HEADS, s=2)
                nc.scalar.copy(out=dst[:, :, :, 0, :], in_=src[:, :, :, 0, :])
                if t >= GROUP - PASSES:
                    sort_words(group + 2, SORTED_TILE, t - (GROUP - PASSES))

                j = part * GROUP + t
                heads = [P, 2, HEADS]
                nc.vector.tensor_tensor(
                    out=dst[:, :, :, 1, :],
                    in0=src[:, :, :, 1, :],
                    in1=cos[:, j, :, :]
                    .rearrange("p i e -> p (i e)")
                    .unsqueeze(1)
                    .unsqueeze(1)
                    .to_broadcast(heads + [ROPE]),
                    op=ALU.mult,
                )
                src_pairs = src[:, :, :, 1, :].rearrange("p q h (i e) -> p q h i e", e=2)
                cross = cross_pool.tile([P, 2, HEADS, FREQS, 2], F32, name="cross")
                nc.vector.tensor_tensor(
                    out=cross[:],
                    in0=src_pairs[:, :, :, :, ::-1],
                    in1=signed_sin[:, j, :, :]
                    .unsqueeze(1)
                    .unsqueeze(1)
                    .to_broadcast(heads + [FREQS, 2]),
                    op=ALU.mult,
                )
                if t < gpsimd_adds:
                    nc.gpsimd.tensor_tensor(
                        out=dst[:, :, :, 1, :],
                        in0=dst[:, :, :, 1, :],
                        in1=cross[:].rearrange("p q h i e -> p q h (i e)"),
                        op=ALU.add,
                    )
                    if last_group:
                        store(t, 1)
                else:
                    left_to_add.append((t, dst[:, :, :, 1, :], cross))
            for t, rotated, cross in left_to_add:
                nc.vector.tensor_tensor(
                    out=rotated,
                    in0=rotated,
                    in1=cross[:].rearrange("p q h i e -> p q h (i e)"),
                    op=ALU.add,
                )
                if last_group:
                    store(t, 1)
            if not last_group:
                store(0, GROUP)

        quantised = transpose_and_quantise(0)
        cos, signed_sin = rope_tables(nc, consts, turns_of)
        for group in range(1, GROUPS):
            following = transpose_and_quantise(group)
            if group == 1:
                unread = sums_psum.tile([P, 2 * COLS], F32, name="sums")
                for repeat in range(WARMING_MATMULS):
                    nc.tensor.matmul(
                        out=unread[:],
                        lhsT=x_loaded[0][:, 0, 0:P],
                        rhs=x_loaded[0][:, 0, 0 : 2 * COLS],
                        start=True,
                        stop=True,
                    )
            multiply_and_rotate(group - 1, quantised[0], quantised[1])
            quantised = following
        multiply_and_rotate(GROUPS - 1, quantised[0], quantised[1])
